import numpy as np
import ml_dtypes


def mxq(x, axis, fmt="e4m3"):
    dtype, down = {"e4m3": (ml_dtypes.float8_e4m3fn, 7), "e5m2": (ml_dtypes.float8_e5m2, 14)}[fmt]
    v = np.moveaxis(np.asarray(x, np.float32).astype(ml_dtypes.bfloat16).astype(np.float64), axis, -1)
    blocks = v.reshape(v.shape[:-1] + (-1, 32))
    amax = np.abs(blocks).max(-1, keepdims=True)
    byte = np.maximum(np.where(amax > 0, np.frexp(amax)[1] - 1 + 127, 0) - down, 1)
    scale = np.exp2(byte - 127.0)
    codes = (blocks / scale).astype(np.float32).astype(dtype).astype(np.float64)
    return np.moveaxis((codes * scale).reshape(v.shape), -1, axis)


WIDE = False


def mx_kscale(k):
    if not WIDE:
        return np.ones(k)
    levels = np.array([10, -10, 5, -5, 0])
    if k % 512:
        return np.exp2(np.random.permutation(np.resize(levels, k // 32))).repeat(32)
    a = np.empty((k // 512, 16))
    for p in range(k // 512):
        a[p, :8] = np.random.permutation(np.resize(levels, 8))
        for g in range(8):
            far = levels[np.abs(levels - a[p, g]) >= 10]
            a[p, g + 8] = far[np.random.randint(len(far))]
    return np.exp2(a.ravel()).repeat(32)


BF16 = ml_dtypes.bfloat16


def bf(x):
    return np.asarray(x, np.float32).astype(BF16)


def f64(x):
    return np.asarray(x).astype(np.float64)


B, N, C, H, R, BLK = 8, 256, 1024, 16, 128, 16


def setup_inputs():
    s, t = mx_kscale(C), mx_kscale(C)
    return {"wv": bf(np.random.standard_normal((B, N, C)) * 0.12),
            "x": bf(np.random.standard_normal((B, N, C)) * t),
            "dw_w": bf(np.random.standard_normal(C) * 6.0 * s),
            "dw_b": bf(np.random.standard_normal(C) * 0.4 * s),
            "pw_w": bf(np.random.standard_normal((C, C)) / np.sqrt(C) * t[:, None] / s[None, :]),
            "pw_b": bf(np.random.standard_normal(C) * 0.3 * t),
            "p_w1": bf(np.random.standard_normal((R, C)) / np.sqrt(C) / t[None, :])}


def reference(wv, x, dw_w, dw_b, pw_w, pw_b, p_w1):
    a = f64(wv) * f64(dw_w) + f64(dw_b)
    dyn = (mxq(a, 2, "e4m3") @ mxq(f64(pw_w), 1, "e4m3").T) + f64(pw_b)
    y = dyn + f64(x)
    return mxq(y, 2, "e4m3") @ mxq(f64(p_w1), 1, "e4m3").T

@@ -1,0 +1,310 @@
+import concourse.masks as masks
+import concourse.mybir as mybir
+
+FP8X4 = mybir.dt.float8_e4m3fn_x4
+BF16 = mybir.dt.bfloat16
+F32 = mybir.dt.float32
+U32 = mybir.dt.uint32
+U8 = mybir.dt.uint8
+IDENTITY = mybir.ActivationFunctionType.Identity
+ADD = mybir.AluOpType.add
+
+P = 128
+PACK = 4
+HALF = P * PACK
+PAIR = 2
+TOKENS = 2048
+CHANNELS = 1024
+RANK = 128
+HALVES = CHANNELS // HALF
+CHUNK = 512
+BLOCKS = CHUNK // P
+PART = CHUNK // 2
+CHUNKS = TOKENS // CHUNK
+STEPS = CHUNKS * HALVES
+BANKS = 8
+VECTORS = 3
+
+FLOPS = 2 * TOKENS * CHANNELS * CHANNELS + 2 * TOKENS * CHANNELS * RANK
+
+
+def tile_dssattention_pa_kernel(tc, wv, x, dw_w, dw_b, pw_w, pw_b, p_w1, out):
+    nc = tc.nc
+    wv_rows = wv.flatten_outer_dims()
+    x_rows = x.flatten_outer_dims()
+    out_rows = out.flatten_outer_dims()
+
+    with (
+        tc.tile_pool(name="keep", bufs=1) as keep,
+        tc.tile_pool(name="loads", bufs=STEPS) as loads,
+        tc.tile_pool(name="work", bufs=2) as work,
+        tc.psum_pool(name="psum", bufs=BANKS) as psum,
+        tc.manual_schedule(),
+    ):
+        def load_half(rows, j, tag):
+            i, g = divmod(j, HALVES)
+            half = loads.tile([P, BLOCKS, HALF], BF16, tag=tag, name=tag)
+            nc.sync.dma_start(
+                out=half[:],
+                in_=rows[i * CHUNK : (i + 1) * CHUNK, g * HALF : (g + 1) * HALF].rearrange(
+                    "(p b) c -> p b c", b=BLOCKS
+                ),
+            )
+            return half
+
+        pw_raw = keep.tile([P, HALVES * PACK, CHANNELS], BF16)
+
+        def load_pw(h):
+            nc.sync.dma_start(
+                out=pw_raw[:, h * PACK : (h + 1) * PACK, :],
+                in_=pw_w[h * HALF : (h + 1) * HALF, :].rearrange("(p t) c -> p t c", t=PACK),
+            )
+
+        vector_rows = keep.tile([P, HALF], BF16)
+        nc.vector.memset(vector_rows[:], 0.0)
+        for v, vector in enumerate((dw_w, dw_b, pw_b)):
+            nc.scalar.dma_start(
+                out=vector_rows[v * HALVES : (v + 1) * HALVES, :],
+                in_=vector.rearrange("(g c) -> g c", g=HALVES),
+            )
+
+        p1_raw = keep.tile([P, CHANNELS], BF16)
+        wv_half = {}
+        x_half = {}
+        wv_half[0] = load_half(wv_rows, 0, "wv")
+        wv_half[1] = load_half(wv_rows, 1, "wv")
+        load_pw(0)
+        x_half[0] = load_half(x_rows, 0, "x")
+        wv_half[2] = load_half(wv_rows, 2, "wv")
+        nc.sync.dma_start(out=p1_raw[:], in_=p_w1)
+        wv_half[3] = load_half(wv_rows, 3, "wv")
+        x_half[1] = load_half(x_rows, 1, "x")
+        load_pw(1)
+        for j in range(2, STEPS):
+            if j + 2 < STEPS:
+                wv_half[j + 2] = load_half(wv_rows, j + 2, "wv")
+            x_half[j] = load_half(x_rows, j, "x")
+
+        ident = keep.tile([P, P], F32)
+        masks.make_identity(nc, ident[:])
+
+        def words(raw, g, u):
+            return raw.bitcast(F32)[:, PAIR * P * g + u : PAIR * P * (g + 1) : PAIR]
+
+        def transpose_words(word_blocks):
+            bank = psum.tile([P, CHUNK], F32, tag="bank", name="bank")
+            for n, block in enumerate(word_blocks):
+                nc.tensor.transpose(bank[:, n * P : (n + 1) * P], block, ident[:])
+            return bank
+
+        vector_bank = transpose_words([words(vector_rows[:], 0, u) for u in range(PAIR)])
+        vectors = keep.tile([P, VECTORS, HALVES * PACK], F32)
+        for u in range(PAIR):
+            nc.vector.tensor_copy(
+                out=vectors[:].rearrange("p v (g u e) -> p (v g) u e", g=HALVES, u=PAIR)[:, :, u, :],
+                in_=vector_bank[:, u * P : u * P + VECTORS * HALVES]
+                .bitcast(BF16)
+                .rearrange("p (r e) -> p r e", e=PAIR),
+            )
+        dww = vectors[:, 0, :]
+        dwb = vectors[:, 1, :]
+        pwb = vectors[:, 2, :]
+
+        def planes_of(half, scale, bias, g, dtype, tag, bufs):
+            planes = work.tile([P, PACK, CHUNK], dtype, tag=tag, name=tag, bufs=bufs)
+            for u in range(PACK // PAIR):
+                bank = transpose_words([words(half[:, b, :], 0, u) for b in range(BLOCKS)])
+                pairs = bank[:].bitcast(BF16).rearrange("p (n e) -> p n e", e=PAIR)
+                for e in range(PAIR):
+                    t = PAIR * u + e
+                    column = slice(g * PACK + t, g * PACK + t + 1)
+                    nc.scalar.activation(
+                        out=planes[:, t, :],
+                        in_=pairs[:, :, e],
+                        func=IDENTITY,
+                        scale=1.0 if scale is None else scale[:, column],
+                        bias=bias[:, column],
+                    )
+            return planes
+
+        def quantise(grouped_bf16, codes, scales):
+            nc.vector.quantize_mx(out=codes.bitcast(FP8X4), scales=scales, in_=grouped_bf16)
+
+        def new_operand(tag):
+            codes = work.tile([P, CHUNK], U32, tag=tag + "_codes", name=tag + "_codes",
+                              bufs=2 * HALVES, align_bytes=64)
+            scales = work.tile([P, CHUNK], U8, tag=tag + "_scales", name=tag + "_scales",
+                               bufs=2 * HALVES, align_bytes=64)
+            return codes, scales
+
+        a_planes = {}
+        a_grouped = {}
+        a_mx = {}
+        xb_planes = {}
+        y_grouped = {}
+        y_mx = {}
+
+        def prep_w(j):
+            a_planes[j] = planes_of(wv_half[j], dww, dwb, j % HALVES, BF16, "a_planes", 3)
+
+        def prep_x(j):
+            xb_planes[j] = planes_of(x_half[j], None, pwb, j % HALVES, F32, "xb_planes", 3)
+
+        def group_w(j):
+            grouped = work.tile([P, CHUNK, PACK], BF16, tag="a_grouped", name="a_grouped",
+                                align_bytes=64)
+            nc.vector.tensor_copy(
+                out=grouped[:].rearrange("p (c i) t -> p c t i", i=4),
+                in_=a_planes[j][:].rearrange("p t (c i) -> p c t i", i=4),
+            )
+            a_grouped[j] = grouped
+
+        def quant_w(j):
+            a_mx[j] = new_operand("a")
+            quantise(a_grouped[j][:].rearrange("p n t -> p (n t)"), a_mx[j][0][:], a_mx[j][1][:])
+
+        pw_codes = keep.tile([P, HALVES, CHANNELS], U32, align_bytes=64)
+        pw_scales = keep.tile([P, HALVES, CHANNELS], U8, align_bytes=64)
+        pw_grouped = {}
+
+        def prep_pw(h, copies):
+            for g in range(HALVES):
+                grouped = work.tile([P, HALF, PAIR], F32, tag="pw_grouped", name="pw_grouped",
+                                    align_bytes=64)
+                for s in range(PACK // PAIR):
+                    bank = transpose_words(
+                        [
+                            words(pw_raw[:, h * PACK + PAIR * s + r, :], g, u)
+                            for u in range(PAIR)
+                            for r in range(PAIR)
+                        ]
+                    )
+                    copies[s](
+                        out=grouped[:, s * PAIR * P : (s + 1) * PAIR * P, :],
+                        in_=bank[:].rearrange("p (u o) -> p o u", u=PAIR),
+                    )
+                pw_grouped[h, g] = grouped
+
+        def quant_pw(h, g):
+            rows = slice(h * HALF, (h + 1) * HALF)
+            quantise(
+                pw_grouped[h, g][:].rearrange("p o u -> p (o u)").bitcast(BF16),
+                pw_codes[:, g, rows],
+                pw_scales[:, g, rows],
+            )
+
+        p1_grouped = keep.tile([P, HALVES, RANK, PAIR], F32, align_bytes=64)
+        p1_codes = keep.tile([P, HALVES, RANK], U32, align_bytes=64)
+        p1_scales = keep.tile([P, HALVES, RANK], U8, align_bytes=64)
+
+        def first_product(k, b):
+            i, h = divmod(k, HALVES)
+            tokens = slice(b * P, (b + 1) * P)
+            bank = psum.tile([P, CHUNK], F32, tag="bank", name="bank")
+            for t in range(PACK):
+                rows = slice((h * PACK + t) * P, (h * PACK + t + 1) * P)
+                for g in range(HALVES):
+                    codes, scales = a_mx[i * HALVES + g]
+                    nc.tensor.matmul_mx(
+                        out=bank[:, t * P : (t + 1) * P],
+                        lhsT=pw_codes[:, g, rows].bitcast(FP8X4),
+                        lhsT_scale=pw_scales[:, g, rows],
+                        rhs=codes[:, tokens].bitcast(FP8X4),
+                        rhs_scale=scales[:, tokens],
+                        start=(g == 0),
+                        stop=(g == HALVES - 1),
+                    )
+            if b == 0:
+                y_grouped[k] = work.tile([P, CHUNK, PACK], BF16, tag="y_grouped", name="y_grouped",
+                                         align_bytes=64)
+            nc.vector.tensor_tensor(
+                out=y_grouped[k][:, tokens, :].rearrange("p (c i) t -> p c t i", i=4),
+                in0=bank[:].rearrange("p (t c i) -> p c t i", t=PACK, i=4),
+                in1=xb_planes[k][:, :, tokens].rearrange("p t (c i) -> p c t i", i=4),
+                op=ADD,
+            )
+
+        def quant_y(k, s):
+            if s == 0:
+                y_mx[k] = new_operand("y")
+            tokens = slice(s * PART, (s + 1) * PART)
+            quantise(
+                y_grouped[k][:, tokens, :].rearrange("p n t -> p (n t)"),
+                y_mx[k][0][:, tokens],
+                y_mx[k][1][:, tokens],
+            )
+
+        def second_product(i, s):
+            bank = psum.tile([P, CHUNK], F32, tag="bank", name="bank")
+            for n in range(PART // P):
+                b = s * (PART // P) + n
+                tokens = slice(b * P, (b + 1) * P)
+                for h in range(HALVES):
+                    codes, scales = y_mx[i * HALVES + h]
+                    nc.tensor.matmul_mx(
+                        out=bank[:, n * RANK : (n + 1) * RANK],
+                        lhsT=codes[:, tokens].bitcast(FP8X4),
+                        lhsT_scale=scales[:, tokens],
+                        rhs=p1_codes[:, h, :].bitcast(FP8X4),
+                        rhs_scale=p1_scales[:, h, :],
+                        start=(h == 0),
+                        stop=(h == HALVES - 1),
+                    )
+            width = (PART // P) * RANK
+            result = work.tile([P, width], F32, tag="result", name="result")
+            nc.scalar.copy(out=result[:], in_=bank[:, :width])
+            nc.sync.dma_start(
+                out=out_rows[i * CHUNK : (i + 1) * CHUNK, :].rearrange(
+                    "(p b) r -> p (b r)", b=BLOCKS
+                )[:, s * width : (s + 1) * width],
+                in_=result[:],
+            )
+
+        prep_w(0)
+        prep_w(1)
+        group_w(0)
+        prep_pw(0, (nc.vector.tensor_copy, nc.vector.tensor_copy))
+        group_w(1)
+        prep_x(0)
+        prep_w(2)
+        p1_bank = transpose_words([words(p1_raw[:], h, u) for h in range(HALVES) for u in range(PAIR)])
+        quant_w(0)
+        quant_pw(0, 0)
+        quant_w(1)
+        nc.vector.tensor_copy(
+            out=p1_grouped[:],
+            in_=p1_bank[:].rearrange("p (h u r) -> p h r u", h=HALVES, u=PAIR),
+        )
+        quant_pw(0, 1)
+        quantise(
+            p1_grouped[:].rearrange("p h r u -> p (h r u)").bitcast(BF16),
+            p1_codes[:].rearrange("p h r -> p (h r)"),
+            p1_scales[:].rearrange("p h r -> p (h r)"),
+        )
+
+        for k in range(STEPS):
+            if k + 2 < STEPS:
+                group_w(k + 2)
+            if k >= 1:
+                quant_y(k - 1, 1)
+            if k + 2 < STEPS:
+                quant_w(k + 2)
+            if k + 3 < STEPS:
+                prep_w(k + 3)
+            first_product(k, 0)
+            first_product(k, 1)
+            if k + 1 < STEPS:
+                prep_x(k + 1)
+            first_product(k, 2)
+            quant_y(k, 0)
+            first_product(k, 3)
+            if k >= HALVES and k % HALVES == 0:
+                second_product(k // HALVES - 1, 0)
+                second_product(k // HALVES - 1, 1)
+            if k + 1 < HALVES:
+                prep_pw(k + 1, (nc.scalar.copy, nc.vector.tensor_copy))
+                quant_pw(k + 1, 0)
+                quant_pw(k + 1, 1)
+        second_product(CHUNKS - 1, 0)
+        quant_y(STEPS - 1, 1)
+        second_product(CHUNKS - 1, 1)

@@ -8,6 +8,7 @@ U32 = mybir.dt.uint32
 U8 = mybir.dt.uint8
 IDENTITY = mybir.ActivationFunctionType.Identity
 ADD = mybir.AluOpType.add
+MULT = mybir.AluOpType.mult
 
 P = 128
 PACK = 4
@@ -63,7 +64,7 @@ def tile_dssattention_pa_kernel(tc, wv, x, dw_w, dw_b, pw_w, pw_b, p_w1, out):
         vector_rows = keep.tile([P, HALF], BF16)
         nc.vector.memset(vector_rows[:], 0.0)
         for v, vector in enumerate((dw_w, dw_b, pw_b)):
-            nc.scalar.dma_start(
+            nc.sync.dma_start(
                 out=vector_rows[v * HALVES : (v + 1) * HALVES, :],
                 in_=vector.rearrange("(g c) -> g c", g=HALVES),
             )
@@ -84,6 +85,10 @@ def tile_dssattention_pa_kernel(tc, wv, x, dw_w, dw_b, pw_w, pw_b, p_w1, out):
             if j + 2 < STEPS:
                 wv_half[j + 2] = load_half(wv_rows, j + 2, "wv")
             x_half[j] = load_half(x_rows, j, "x")
+
+        warm = keep.tile([P, 1], F32)
+        nc.vector.memset(warm[:], 0.0)
+        nc.scalar.activation(out=warm[:], in_=warm[:], func=IDENTITY)
 
         ident = keep.tile([P, P], F32)
         masks.make_identity(nc, ident[:])
@@ -110,7 +115,7 @@ def tile_dssattention_pa_kernel(tc, wv, x, dw_w, dw_b, pw_w, pw_b, p_w1, out):
         dwb = vectors[:, 1, :]
         pwb = vectors[:, 2, :]
 
-        def planes_of(half, scale, bias, g, dtype, tag, bufs):
+        def planes_of(half, scale, bias, g, dtype, tag, bufs, vector_u=None):
             planes = work.tile([P, PACK, CHUNK], dtype, tag=tag, name=tag, bufs=bufs)
             for u in range(PACK // PAIR):
                 bank = transpose_words([words(half[:, b, :], 0, u) for b in range(BLOCKS)])
@@ -118,6 +123,16 @@ def tile_dssattention_pa_kernel(tc, wv, x, dw_w, dw_b, pw_w, pw_b, p_w1, out):
                 for e in range(PAIR):
                     t = PAIR * u + e
                     column = slice(g * PACK + t, g * PACK + t + 1)
+                    if u == vector_u:
+                        nc.vector.tensor_scalar(
+                            out=planes[:, t, :],
+                            in0=pairs[:, :, e],
+                            scalar1=scale[:, column],
+                            scalar2=bias[:, column],
+                            op0=MULT,
+                            op1=ADD,
+                        )
+                        continue
                     nc.scalar.activation(
                         out=planes[:, t, :],
                         in_=pairs[:, :, e],
@@ -144,8 +159,10 @@ def tile_dssattention_pa_kernel(tc, wv, x, dw_w, dw_b, pw_w, pw_b, p_w1, out):
         y_grouped = {}
         y_mx = {}
 
-        def prep_w(j):
-            a_planes[j] = planes_of(wv_half[j], dww, dwb, j % HALVES, BF16, "a_planes", 3)
+        def prep_w(j, vector_u=None):
+            a_planes[j] = planes_of(
+                wv_half[j], dww, dwb, j % HALVES, BF16, "a_planes", 3, vector_u
+            )
 
         def prep_x(j):
             xb_planes[j] = planes_of(x_half[j], None, pwb, j % HALVES, F32, "xb_planes", 3)
@@ -260,22 +277,22 @@ def tile_dssattention_pa_kernel(tc, wv, x, dw_w, dw_b, pw_w, pw_b, p_w1, out):
                 in_=result[:],
             )
 
-        prep_w(0)
-        prep_w(1)
+        prep_w(0, vector_u=1)
+        prep_w(1, vector_u=1)
         group_w(0)
-        prep_pw(0, (nc.vector.tensor_copy, nc.vector.tensor_copy))
+        prep_pw(0, (nc.scalar.copy, nc.vector.tensor_copy))
         group_w(1)
-        prep_x(0)
-        prep_w(2)
-        p1_bank = transpose_words([words(p1_raw[:], h, u) for h in range(HALVES) for u in range(PAIR)])
         quant_w(0)
+        prep_x(0)
         quant_pw(0, 0)
         quant_w(1)
-        nc.vector.tensor_copy(
+        p1_bank = transpose_words([words(p1_raw[:], h, u) for h in range(HALVES) for u in range(PAIR)])
+        nc.scalar.copy(
             out=p1_grouped[:],
             in_=p1_bank[:].rearrange("p (h u r) -> p h r u", h=HALVES, u=PAIR),
         )
         quant_pw(0, 1)
+        prep_w(2)
         quantise(
             p1_grouped[:].rearrange("p h r u -> p (h r u)").bitcast(BF16),
             p1_codes[:].rearrange("p h r -> p (h r)"),

@@ -308,10 +308,10 @@ def tile_dssattention_pa_kernel(tc, wv, x, dw_w, dw_b, pw_w, pw_b, p_w1, out):
                 quant_w(k + 2)
             if k + 3 < STEPS:
                 prep_w(k + 3)
-            first_product(k, 0)
-            first_product(k, 1)
             if k + 1 < STEPS:
                 prep_x(k + 1)
+            first_product(k, 0)
+            first_product(k, 1)
             first_product(k, 2)
             quant_y(k, 0)
             first_product(k, 3)

@@ -61,6 +61,10 @@ def tile_dssattention_pa_kernel(tc, wv, x, dw_w, dw_b, pw_w, pw_b, p_w1, out):
                 in_=pw_w[h * HALF : (h + 1) * HALF, :].rearrange("(p t) c -> p t c", t=PACK),
             )
 
+        p1_raw = keep.tile([P, CHANNELS], BF16)
+        wv_half = {}
+        x_half = {}
+        wv_half[0] = load_half(wv_rows, 0, "wv")
         vector_rows = keep.tile([P, HALF], BF16)
         nc.vector.memset(vector_rows[:], 0.0)
         for v, vector in enumerate((dw_w, dw_b, pw_b)):
@@ -69,10 +73,6 @@ def tile_dssattention_pa_kernel(tc, wv, x, dw_w, dw_b, pw_w, pw_b, p_w1, out):
                 in_=vector.rearrange("(g c) -> g c", g=HALVES),
             )
 
-        p1_raw = keep.tile([P, CHANNELS], BF16)
-        wv_half = {}
-        x_half = {}
-        wv_half[0] = load_half(wv_rows, 0, "wv")
         wv_half[1] = load_half(wv_rows, 1, "wv")
         load_pw(0)
         x_half[0] = load_half(x_rows, 0, "x")
@@ -292,7 +292,7 @@ def tile_dssattention_pa_kernel(tc, wv, x, dw_w, dw_b, pw_w, pw_b, p_w1, out):
             in_=p1_bank[:].rearrange("p (h u r) -> p h r u", h=HALVES, u=PAIR),
         )
         quant_pw(0, 1)
-        prep_w(2)
+        prep_w(2, vector_u=1)
         quantise(
             p1_grouped[:].rearrange("p h r u -> p (h r u)").bitcast(BF16),
             p1_codes[:].rearrange("p h r -> p (h r)"),

@@ -56,10 +56,11 @@ def tile_dssattention_pa_kernel(tc, wv, x, dw_w, dw_b, pw_w, pw_b, p_w1, out):
         pw_raw = keep.tile([P, HALVES * PACK, CHANNELS], BF16)
 
         def load_pw(h):
-            nc.sync.dma_start(
-                out=pw_raw[:, h * PACK : (h + 1) * PACK, :],
-                in_=pw_w[h * HALF : (h + 1) * HALF, :].rearrange("(p t) c -> p t c", t=PACK),
-            )
+            rows = pw_w[h * HALF : (h + 1) * HALF, :].rearrange("(p t) c -> p t c", t=PACK)
+            for t in range(0, PACK, PAIR):
+                nc.sync.dma_start(
+                    out=pw_raw[:, h * PACK + t : h * PACK + t + PAIR, :], in_=rows[:, t : t + PAIR, :]
+                )
 
         p1_raw = keep.tile([P, CHANNELS], BF16)
         wv_half = {}
@@ -186,9 +187,10 @@ def tile_dssattention_pa_kernel(tc, wv, x, dw_w, dw_b, pw_w, pw_b, p_w1, out):
 
         def prep_pw(h, copies):
             for g in range(HALVES):
-                grouped = work.tile([P, HALF, PAIR], F32, tag="pw_grouped", name="pw_grouped",
-                                    align_bytes=64)
-                for s in range(PACK // PAIR):
+                pw_grouped[h, g] = work.tile([P, HALF, PAIR], F32, tag="pw_grouped",
+                                             name="pw_grouped", align_bytes=64)
+            for s in range(PACK // PAIR):
+                for g in range(HALVES):
                     bank = transpose_words(
                         [
                             words(pw_raw[:, h * PACK + PAIR * s + r, :], g, u)
@@ -196,11 +198,10 @@ def tile_dssattention_pa_kernel(tc, wv, x, dw_w, dw_b, pw_w, pw_b, p_w1, out):
                             for r in range(PAIR)
                         ]
                     )
-                    copies[s](
-                        out=grouped[:, s * PAIR * P : (s + 1) * PAIR * P, :],
+                    copies[g](
+                        out=pw_grouped[h, g][:, s * PAIR * P : (s + 1) * PAIR * P, :],
                         in_=bank[:].rearrange("p (u o) -> p o u", u=PAIR),
                     )
-                pw_grouped[h, g] = grouped
 
         def quant_pw(h, g):
             rows = slice(h * HALF, (h + 1) * HALF)
@@ -241,20 +242,19 @@ def tile_dssattention_pa_kernel(tc, wv, x, dw_w, dw_b, pw_w, pw_b, p_w1, out):
                 op=ADD,
             )
 
-        def quant_y(k, s):
-            if s == 0:
+        def quant_y(k, first, last):
+            if first == 0:
                 y_mx[k] = new_operand("y")
-            tokens = slice(s * PART, (s + 1) * PART)
+            tokens = slice(first * P, last * P)
             quantise(
                 y_grouped[k][:, tokens, :].rearrange("p n t -> p (n t)"),
                 y_mx[k][0][:, tokens],
                 y_mx[k][1][:, tokens],
             )
 
-        def second_product(i, s):
+        def second_product(i, first, last):
             bank = psum.tile([P, CHUNK], F32, tag="bank", name="bank")
-            for n in range(PART // P):
-                b = s * (PART // P) + n
+            for n, b in enumerate(range(first, last)):
                 tokens = slice(b * P, (b + 1) * P)
                 for h in range(HALVES):
                     codes, scales = y_mx[i * HALVES + h]
@@ -267,31 +267,31 @@ def tile_dssattention_pa_kernel(tc, wv, x, dw_w, dw_b, pw_w, pw_b, p_w1, out):
                         start=(h == 0),
                         stop=(h == HALVES - 1),
                     )
-            width = (PART // P) * RANK
-            result = work.tile([P, width], F32, tag="result", name="result")
-            nc.scalar.copy(out=result[:], in_=bank[:, :width])
+            width = (last - first) * RANK
+            result = work.tile([P, CHUNK], F32, tag="result", name="result", bufs=4)
+            nc.scalar.copy(out=result[:, :width], in_=bank[:, :width])
             nc.sync.dma_start(
                 out=out_rows[i * CHUNK : (i + 1) * CHUNK, :].rearrange(
                     "(p b) r -> p (b r)", b=BLOCKS
-                )[:, s * width : (s + 1) * width],
-                in_=result[:],
+                )[:, first * RANK : last * RANK],
+                in_=result[:, :width],
             )
 
         prep_w(0, vector_u=1)
-        prep_w(1, vector_u=1)
+        prep_w(1)
         group_w(0)
         prep_pw(0, (nc.scalar.copy, nc.vector.tensor_copy))
         group_w(1)
         quant_w(0)
+        quant_w(1)
         prep_x(0)
         quant_pw(0, 0)
-        quant_w(1)
+        quant_pw(0, 1)
         p1_bank = transpose_words([words(p1_raw[:], h, u) for h in range(HALVES) for u in range(PAIR)])
         nc.scalar.copy(
             out=p1_grouped[:],
             in_=p1_bank[:].rearrange("p (h u r) -> p h r u", h=HALVES, u=PAIR),
         )
-        quant_pw(0, 1)
         prep_w(2, vector_u=1)
         quantise(
             p1_grouped[:].rearrange("p h r u -> p (h r u)").bitcast(BF16),
@@ -303,25 +303,25 @@ def tile_dssattention_pa_kernel(tc, wv, x, dw_w, dw_b, pw_w, pw_b, p_w1, out):
             if k + 2 < STEPS:
                 group_w(k + 2)
             if k >= 1:
-                quant_y(k - 1, 1)
+                quant_y(k - 1, 2, BLOCKS)
             if k + 2 < STEPS:
                 quant_w(k + 2)
             if k + 3 < STEPS:
                 prep_w(k + 3)
             if k + 1 < STEPS:
                 prep_x(k + 1)
-            first_product(k, 0)
-            first_product(k, 1)
-            first_product(k, 2)
-            quant_y(k, 0)
-            first_product(k, 3)
+            for b in range(BLOCKS):
+                first_product(k, b)
+                if b == 2:
+                    quant_y(k, 0, 2)
             if k >= HALVES and k % HALVES == 0:
-                second_product(k // HALVES - 1, 0)
-                second_product(k // HALVES - 1, 1)
+                second_product(k // HALVES - 1, 0, BLOCKS)
             if k + 1 < HALVES:
-                prep_pw(k + 1, (nc.scalar.copy, nc.vector.tensor_copy))
+                prep_pw(k + 1, (nc.scalar.copy, nc.scalar.copy))
                 quant_pw(k + 1, 0)
                 quant_pw(k + 1, 1)
-        second_product(CHUNKS - 1, 0)
-        quant_y(STEPS - 1, 1)
-        second_product(CHUNKS - 1, 1)
+        second_product(CHUNKS - 1, 0, 2)
+        quant_y(STEPS - 1, 2, 3)
+        quant_y(STEPS - 1, 3, 4)
+        second_product(CHUNKS - 1, 2, 3)
+        second_product(CHUNKS - 1, 3, 4)

@@ -42,15 +42,15 @@ def tile_dssattention_pa_kernel(tc, wv, x, dw_w, dw_b, pw_w, pw_b, p_w1, out):
         tc.psum_pool(name="psum", bufs=BANKS) as psum,
         tc.manual_schedule(),
     ):
-        def load_half(rows, j, tag):
+        def load_half(rows, j, tag, pieces=1):
             i, g = divmod(j, HALVES)
             half = loads.tile([P, BLOCKS, HALF], BF16, tag=tag, name=tag)
-            nc.sync.dma_start(
-                out=half[:],
-                in_=rows[i * CHUNK : (i + 1) * CHUNK, g * HALF : (g + 1) * HALF].rearrange(
-                    "(p b) c -> p b c", b=BLOCKS
-                ),
+            source = rows[i * CHUNK : (i + 1) * CHUNK, g * HALF : (g + 1) * HALF].rearrange(
+                "(p b) c -> p b c", b=BLOCKS
             )
+            step = BLOCKS // pieces
+            for b in range(0, BLOCKS, step):
+                nc.sync.dma_start(out=half[:, b : b + step, :], in_=source[:, b : b + step, :])
             return half
 
         pw_raw = keep.tile([P, HALVES * PACK, CHANNELS], BF16)
@@ -65,7 +65,7 @@ def tile_dssattention_pa_kernel(tc, wv, x, dw_w, dw_b, pw_w, pw_b, p_w1, out):
         p1_raw = keep.tile([P, CHANNELS], BF16)
         wv_half = {}
         x_half = {}
-        wv_half[0] = load_half(wv_rows, 0, "wv")
+        wv_half[0] = load_half(wv_rows, 0, "wv", pieces=2)
         vector_rows = keep.tile([P, HALF], BF16)
         nc.vector.memset(vector_rows[:], 0.0)
         for v, vector in enumerate((dw_w, dw_b, pw_b)):
@@ -78,10 +78,10 @@ def tile_dssattention_pa_kernel(tc, wv, x, dw_w, dw_b, pw_w, pw_b, p_w1, out):
         load_pw(0)
         x_half[0] = load_half(x_rows, 0, "x")
         wv_half[2] = load_half(wv_rows, 2, "wv")
-        nc.sync.dma_start(out=p1_raw[:], in_=p_w1)
         wv_half[3] = load_half(wv_rows, 3, "wv")
         x_half[1] = load_half(x_rows, 1, "x")
         load_pw(1)
+        nc.sync.dma_start(out=p1_raw[:], in_=p_w1)
         for j in range(2, STEPS):
             if j + 2 < STEPS:
                 wv_half[j + 2] = load_half(wv_rows, j + 2, "wv")
@@ -116,17 +116,22 @@ def tile_dssattention_pa_kernel(tc, wv, x, dw_w, dw_b, pw_w, pw_b, p_w1, out):
         dwb = vectors[:, 1, :]
         pwb = vectors[:, 2, :]
 
-        def planes_of(half, scale, bias, g, dtype, tag, bufs, vector_u=None):
+        def planes_of(half, scale, bias, g, dtype, tag, bufs, vector_u=None, by_blocks=False):
             planes = work.tile([P, PACK, CHUNK], dtype, tag=tag, name=tag, bufs=bufs)
-            for u in range(PACK // PAIR):
-                bank = transpose_words([words(half[:, b, :], 0, u) for b in range(BLOCKS)])
-                pairs = bank[:].bitcast(BF16).rearrange("p (n e) -> p n e", e=PAIR)
-                for e in range(PAIR):
+            us = range(PACK // PAIR)
+            for v in range(2):
+                bank_us = us if by_blocks else (v,)
+                bank_blocks = range(v * BLOCKS // 2, (v + 1) * BLOCKS // 2) if by_blocks else range(BLOCKS)
+                tokens = slice(bank_blocks[0] * P, (bank_blocks[-1] + 1) * P)
+                bank = transpose_words([words(half[:, b, :], 0, u) for u in bank_us for b in bank_blocks])
+                all_pairs = bank[:].bitcast(BF16).rearrange("p (u n e) -> p u n e", u=len(bank_us), e=PAIR)
+                for u, e in [(u, e) for u in bank_us for e in range(PAIR)]:
                     t = PAIR * u + e
+                    pairs = all_pairs[:, u - bank_us[0]]
                     column = slice(g * PACK + t, g * PACK + t + 1)
-                    if u == vector_u:
+                    if v == vector_u:
                         nc.vector.tensor_scalar(
-                            out=planes[:, t, :],
+                            out=planes[:, t, tokens],
                             in0=pairs[:, :, e],
                             scalar1=scale[:, column],
                             scalar2=bias[:, column],
@@ -135,7 +140,7 @@ def tile_dssattention_pa_kernel(tc, wv, x, dw_w, dw_b, pw_w, pw_b, p_w1, out):
                         )
                         continue
                     nc.scalar.activation(
-                        out=planes[:, t, :],
+                        out=planes[:, t, tokens],
                         in_=pairs[:, :, e],
                         func=IDENTITY,
                         scale=1.0 if scale is None else scale[:, column],
@@ -160,9 +165,9 @@ def tile_dssattention_pa_kernel(tc, wv, x, dw_w, dw_b, pw_w, pw_b, p_w1, out):
         y_grouped = {}
         y_mx = {}
 
-        def prep_w(j, vector_u=None):
+        def prep_w(j, vector_u=None, by_blocks=False):
             a_planes[j] = planes_of(
-                wv_half[j], dww, dwb, j % HALVES, BF16, "a_planes", 3, vector_u
+                wv_half[j], dww, dwb, j % HALVES, BF16, "a_planes", 3, vector_u, by_blocks
             )
 
         def prep_x(j):
@@ -277,7 +282,7 @@ def tile_dssattention_pa_kernel(tc, wv, x, dw_w, dw_b, pw_w, pw_b, p_w1, out):
                 in_=result[:, :width],
             )
 
-        prep_w(0, vector_u=1)
+        prep_w(0, vector_u=1, by_blocks=True)
         prep_w(1)
         group_w(0)
         prep_pw(0, (nc.scalar.copy, nc.vector.tensor_copy))
@@ -287,17 +292,7 @@ def tile_dssattention_pa_kernel(tc, wv, x, dw_w, dw_b, pw_w, pw_b, p_w1, out):
         prep_x(0)
         quant_pw(0, 0)
         quant_pw(0, 1)
-        p1_bank = transpose_words([words(p1_raw[:], h, u) for h in range(HALVES) for u in range(PAIR)])
-        nc.scalar.copy(
-            out=p1_grouped[:],
-            in_=p1_bank[:].rearrange("p (h u r) -> p h r u", h=HALVES, u=PAIR),
-        )
         prep_w(2, vector_u=1)
-        quantise(
-            p1_grouped[:].rearrange("p h r u -> p (h r u)").bitcast(BF16),
-            p1_codes[:].rearrange("p h r -> p (h r)"),
-            p1_scales[:].rearrange("p h r -> p (h r)"),
-        )
 
         for k in range(STEPS):
             if k + 2 < STEPS:
@@ -316,6 +311,17 @@ def tile_dssattention_pa_kernel(tc, wv, x, dw_w, dw_b, pw_w, pw_b, p_w1, out):
                     quant_y(k, 0, 2)
             if k >= HALVES and k % HALVES == 0:
                 second_product(k // HALVES - 1, 0, BLOCKS)
+            if k == 1:
+                p1_bank = transpose_words([words(p1_raw[:], h, u) for h in range(HALVES) for u in range(PAIR)])
+                nc.scalar.copy(
+                    out=p1_grouped[:],
+                    in_=p1_bank[:].rearrange("p (h u r) -> p h r u", h=HALVES, u=PAIR),
+                )
+                quantise(
+                    p1_grouped[:].rearrange("p h r u -> p (h r u)").bitcast(BF16),
+                    p1_codes[:].rearrange("p h r -> p (h r)"),
+                    p1_scales[:].rearrange("p h r -> p (h r)"),
+                )
             if k + 1 < HALVES:
                 prep_pw(k + 1, (nc.scalar.copy, nc.scalar.copy))
                 quant_pw(k + 1, 0)

@@ -307,6 +307,8 @@ def tile_dssattention_pa_kernel(tc, wv, x, dw_w, dw_b, pw_w, pw_b, p_w1, out):
                 prep_x(k + 1)
             for b in range(BLOCKS):
                 first_product(k, b)
+                if k == 0 and b == 0:
+                    prep_pw(1, (nc.scalar.copy, nc.scalar.copy))
                 if b == 2:
                     quant_y(k, 0, 2)
             if k >= HALVES and k % HALVES == 0:
@@ -322,10 +324,9 @@ def tile_dssattention_pa_kernel(tc, wv, x, dw_w, dw_b, pw_w, pw_b, p_w1, out):
                     p1_codes[:].rearrange("p h r -> p (h r)"),
                     p1_scales[:].rearrange("p h r -> p (h r)"),
                 )
-            if k + 1 < HALVES:
-                prep_pw(k + 1, (nc.scalar.copy, nc.scalar.copy))
-                quant_pw(k + 1, 0)
-                quant_pw(k + 1, 1)
+            if k == 0:
+                quant_pw(1, 0)
+                quant_pw(1, 1)
         second_product(CHUNKS - 1, 0, 2)
         quant_y(STEPS - 1, 2, 3)
         quant_y(STEPS - 1, 3, 4)

@@ -177,8 +177,8 @@ def tile_dssattention_pa_kernel(tc, wv, x, dw_w, dw_b, pw_w, pw_b, p_w1, out):
             grouped = work.tile([P, CHUNK, PACK], BF16, tag="a_grouped", name="a_grouped",
                                 align_bytes=64)
             nc.vector.tensor_copy(
-                out=grouped[:].rearrange("p (c i) t -> p c t i", i=4),
-                in_=a_planes[j][:].rearrange("p t (c i) -> p c t i", i=4),
+                out=grouped[:].rearrange("p (c i) t -> p c t i", i=8),
+                in_=a_planes[j][:].rearrange("p t (c i) -> p c t i", i=8),
             )
             a_grouped[j] = grouped
 

import concourse.masks as masks
import concourse.mybir as mybir

FP8X4 = mybir.dt.float8_e4m3fn_x4
BF16 = mybir.dt.bfloat16
F32 = mybir.dt.float32
U32 = mybir.dt.uint32
U8 = mybir.dt.uint8
IDENTITY = mybir.ActivationFunctionType.Identity
ADD = mybir.AluOpType.add
MULT = mybir.AluOpType.mult

P = 128
PACK = 4
HALF = P * PACK
PAIR = 2
TOKENS = 2048
CHANNELS = 1024
RANK = 128
HALVES = CHANNELS // HALF
CHUNK = 512
BLOCKS = CHUNK // P
PART = CHUNK // 2
CHUNKS = TOKENS // CHUNK
STEPS = CHUNKS * HALVES
BANKS = 8
VECTORS = 3

FLOPS = 2 * TOKENS * CHANNELS * CHANNELS + 2 * TOKENS * CHANNELS * RANK


def tile_dssattention_pa_kernel(tc, wv, x, dw_w, dw_b, pw_w, pw_b, p_w1, out):
    nc = tc.nc
    wv_rows = wv.flatten_outer_dims()
    x_rows = x.flatten_outer_dims()
    out_rows = out.flatten_outer_dims()

    with (
        tc.tile_pool(name="keep", bufs=1) as keep,
        tc.tile_pool(name="loads", bufs=STEPS) as loads,
        tc.tile_pool(name="work", bufs=2) as work,
        tc.psum_pool(name="psum", bufs=BANKS) as psum,
        tc.manual_schedule(),
    ):
        def load_half(rows, j, tag, pieces=1):
            i, g = divmod(j, HALVES)
            half = loads.tile([P, BLOCKS, HALF], BF16, tag=tag, name=tag)
            source = rows[i * CHUNK : (i + 1) * CHUNK, g * HALF : (g + 1) * HALF].rearrange(
                "(p b) c -> p b c", b=BLOCKS
            )
            step = BLOCKS // pieces
            for b in range(0, BLOCKS, step):
                nc.sync.dma_start(out=half[:, b : b + step, :], in_=source[:, b : b + step, :])
            return half

        pw_raw = keep.tile([P, HALVES * PACK, CHANNELS], BF16)

        def load_pw(h):
            rows = pw_w[h * HALF : (h + 1) * HALF, :].rearrange("(p t) c -> p t c", t=PACK)
            for t in range(0, PACK, PAIR):
                nc.sync.dma_start(
                    out=pw_raw[:, h * PACK + t : h * PACK + t + PAIR, :], in_=rows[:, t : t + PAIR, :]
                )

        p1_raw = keep.tile([P, CHANNELS], BF16)
        wv_half = {}
        x_half = {}
        wv_half[0] = load_half(wv_rows, 0, "wv", pieces=2)
        vector_rows = keep.tile([P, HALF], BF16)
        nc.vector.memset(vector_rows[:], 0.0)
        for v, vector in enumerate((dw_w, dw_b, pw_b)):
            nc.sync.dma_start(
                out=vector_rows[v * HALVES : (v + 1) * HALVES, :],
                in_=vector.rearrange("(g c) -> g c", g=HALVES),
            )

        wv_half[1] = load_half(wv_rows, 1, "wv")
        load_pw(0)
        x_half[0] = load_half(x_rows, 0, "x")
        wv_half[2] = load_half(wv_rows, 2, "wv")
        wv_half[3] = load_half(wv_rows, 3, "wv")
        x_half[1] = load_half(x_rows, 1, "x")
        load_pw(1)
        nc.sync.dma_start(out=p1_raw[:], in_=p_w1)
        for j in range(2, STEPS):
            if j + 2 < STEPS:
                wv_half[j + 2] = load_half(wv_rows, j + 2, "wv")
            x_half[j] = load_half(x_rows, j, "x")

        warm = keep.tile([P, 1], F32)
        nc.vector.memset(warm[:], 0.0)
        nc.scalar.activation(out=warm[:], in_=warm[:], func=IDENTITY)

        ident = keep.tile([P, P], F32)
        masks.make_identity(nc, ident[:])

        def words(raw, g, u):
            return raw.bitcast(F32)[:, PAIR * P * g + u : PAIR * P * (g + 1) : PAIR]

        def transpose_words(word_blocks):
            bank = psum.tile([P, CHUNK], F32, tag="bank", name="bank")
            for n, block in enumerate(word_blocks):
                nc.tensor.transpose(bank[:, n * P : (n + 1) * P], block, ident[:])
            return bank

        vector_bank = transpose_words([words(vector_rows[:], 0, u) for u in range(PAIR)])
        vectors = keep.tile([P, VECTORS, HALVES * PACK], F32)
        for u in range(PAIR):
            nc.vector.tensor_copy(
                out=vectors[:].rearrange("p v (g u e) -> p (v g) u e", g=HALVES, u=PAIR)[:, :, u, :],
                in_=vector_bank[:, u * P : u * P + VECTORS * HALVES]
                .bitcast(BF16)
                .rearrange("p (r e) -> p r e", e=PAIR),
            )
        dww = vectors[:, 0, :]
        dwb = vectors[:, 1, :]
        pwb = vectors[:, 2, :]

        def planes_of(half, scale, bias, g, dtype, tag, bufs, vector_u=None, by_blocks=False):
            planes = work.tile([P, PACK, CHUNK], dtype, tag=tag, name=tag, bufs=bufs)
            us = range(PACK // PAIR)
            for v in range(2):
                bank_us = us if by_blocks else (v,)
                bank_blocks = range(v * BLOCKS // 2, (v + 1) * BLOCKS // 2) if by_blocks else range(BLOCKS)
                tokens = slice(bank_blocks[0] * P, (bank_blocks[-1] + 1) * P)
                bank = transpose_words([words(half[:, b, :], 0, u) for u in bank_us for b in bank_blocks])
                all_pairs = bank[:].bitcast(BF16).rearrange("p (u n e) -> p u n e", u=len(bank_us), e=PAIR)
                for u, e in [(u, e) for u in bank_us for e in range(PAIR)]:
                    t = PAIR * u + e
                    pairs = all_pairs[:, u - bank_us[0]]
                    column = slice(g * PACK + t, g * PACK + t + 1)
                    if v == vector_u:
                        nc.vector.tensor_scalar(
                            out=planes[:, t, tokens],
                            in0=pairs[:, :, e],
                            scalar1=scale[:, column],
                            scalar2=bias[:, column],
                            op0=MULT,
                            op1=ADD,
                        )
                        continue
                    nc.scalar.activation(
                        out=planes[:, t, tokens],
                        in_=pairs[:, :, e],
                        func=IDENTITY,
                        scale=1.0 if scale is None else scale[:, column],
                        bias=bias[:, column],
                    )
            return planes

        def quantise(grouped_bf16, codes, scales):
            nc.vector.quantize_mx(out=codes.bitcast(FP8X4), scales=scales, in_=grouped_bf16)

        def new_operand(tag):
            codes = work.tile([P, CHUNK], U32, tag=tag + "_codes", name=tag + "_codes",
                              bufs=2 * HALVES, align_bytes=64)
            scales = work.tile([P, CHUNK], U8, tag=tag + "_scales", name=tag + "_scales",
                               bufs=2 * HALVES, align_bytes=64)
            return codes, scales

        a_planes = {}
        a_grouped = {}
        a_mx = {}
        xb_planes = {}
        y_grouped = {}
        y_mx = {}

        def prep_w(j, vector_u=None, by_blocks=False):
            a_planes[j] = planes_of(
                wv_half[j], dww, dwb, j % HALVES, BF16, "a_planes", 3, vector_u, by_blocks
            )

        def prep_x(j):
            xb_planes[j] = planes_of(x_half[j], None, pwb, j % HALVES, F32, "xb_planes", 3)

        def group_w(j):
            grouped = work.tile([P, CHUNK, PACK], BF16, tag="a_grouped", name="a_grouped",
                                align_bytes=64)
            nc.vector.tensor_copy(
                out=grouped[:].rearrange("p (c i) t -> p c t i", i=8),
                in_=a_planes[j][:].rearrange("p t (c i) -> p c t i", i=8),
            )
            a_grouped[j] = grouped

        def quant_w(j):
            a_mx[j] = new_operand("a")
            quantise(a_grouped[j][:].rearrange("p n t -> p (n t)"), a_mx[j][0][:], a_mx[j][1][:])

        pw_codes = keep.tile([P, HALVES, CHANNELS], U32, align_bytes=64)
        pw_scales = keep.tile([P, HALVES, CHANNELS], U8, align_bytes=64)
        pw_grouped = {}

        def prep_pw(h, copies):
            for g in range(HALVES):
                pw_grouped[h, g] = work.tile([P, HALF, PAIR], F32, tag="pw_grouped",
                                             name="pw_grouped", align_bytes=64)
            for s in range(PACK // PAIR):
                for g in range(HALVES):
                    bank = transpose_words(
                        [
                            words(pw_raw[:, h * PACK + PAIR * s + r, :], g, u)
                            for u in range(PAIR)
                            for r in range(PAIR)
                        ]
                    )
                    copies[g](
                        out=pw_grouped[h, g][:, s * PAIR * P : (s + 1) * PAIR * P, :],
                        in_=bank[:].rearrange("p (u o) -> p o u", u=PAIR),
                    )

        def quant_pw(h, g):
            rows = slice(h * HALF, (h + 1) * HALF)
            quantise(
                pw_grouped[h, g][:].rearrange("p o u -> p (o u)").bitcast(BF16),
                pw_codes[:, g, rows],
                pw_scales[:, g, rows],
            )

        p1_grouped = keep.tile([P, HALVES, RANK, PAIR], F32, align_bytes=64)
        p1_codes = keep.tile([P, HALVES, RANK], U32, align_bytes=64)
        p1_scales = keep.tile([P, HALVES, RANK], U8, align_bytes=64)

        def first_product(k, b):
            i, h = divmod(k, HALVES)
            tokens = slice(b * P, (b + 1) * P)
            bank = psum.tile([P, CHUNK], F32, tag="bank", name="bank")
            for t in range(PACK):
                rows = slice((h * PACK + t) * P, (h * PACK + t + 1) * P)
                for g in range(HALVES):
                    codes, scales = a_mx[i * HALVES + g]
                    nc.tensor.matmul_mx(
                        out=bank[:, t * P : (t + 1) * P],
                        lhsT=pw_codes[:, g, rows].bitcast(FP8X4),
                        lhsT_scale=pw_scales[:, g, rows],
                        rhs=codes[:, tokens].bitcast(FP8X4),
                        rhs_scale=scales[:, tokens],
                        start=(g == 0),
                        stop=(g == HALVES - 1),
                    )
            if b == 0:
                y_grouped[k] = work.tile([P, CHUNK, PACK], BF16, tag="y_grouped", name="y_grouped",
                                         align_bytes=64)
            nc.vector.tensor_tensor(
                out=y_grouped[k][:, tokens, :].rearrange("p (c i) t -> p c t i", i=4),
                in0=bank[:].rearrange("p (t c i) -> p c t i", t=PACK, i=4),
                in1=xb_planes[k][:, :, tokens].rearrange("p t (c i) -> p c t i", i=4),
                op=ADD,
            )

        def quant_y(k, first, last):
            if first == 0:
                y_mx[k] = new_operand("y")
            tokens = slice(first * P, last * P)
            quantise(
                y_grouped[k][:, tokens, :].rearrange("p n t -> p (n t)"),
                y_mx[k][0][:, tokens],
                y_mx[k][1][:, tokens],
            )

        def second_product(i, first, last):
            bank = psum.tile([P, CHUNK], F32, tag="bank", name="bank")
            for n, b in enumerate(range(first, last)):
                tokens = slice(b * P, (b + 1) * P)
                for h in range(HALVES):
                    codes, scales = y_mx[i * HALVES + h]
                    nc.tensor.matmul_mx(
                        out=bank[:, n * RANK : (n + 1) * RANK],
                        lhsT=codes[:, tokens].bitcast(FP8X4),
                        lhsT_scale=scales[:, tokens],
                        rhs=p1_codes[:, h, :].bitcast(FP8X4),
                        rhs_scale=p1_scales[:, h, :],
                        start=(h == 0),
                        stop=(h == HALVES - 1),
                    )
            width = (last - first) * RANK
            result = work.tile([P, CHUNK], F32, tag="result", name="result", bufs=4)
            nc.scalar.copy(out=result[:, :width], in_=bank[:, :width])
            nc.sync.dma_start(
                out=out_rows[i * CHUNK : (i + 1) * CHUNK, :].rearrange(
                    "(p b) r -> p (b r)", b=BLOCKS
                )[:, first * RANK : last * RANK],
                in_=result[:, :width],
            )

        prep_w(0, vector_u=1, by_blocks=True)
        prep_w(1)
        group_w(0)
        prep_pw(0, (nc.scalar.copy, nc.vector.tensor_copy))
        group_w(1)
        quant_w(0)
        quant_w(1)
        prep_x(0)
        quant_pw(0, 0)
        quant_pw(0, 1)
        prep_w(2, vector_u=1)

        for k in range(STEPS):
            if k + 2 < STEPS:
                group_w(k + 2)
            if k >= 1:
                quant_y(k - 1, 2, BLOCKS)
            if k + 2 < STEPS:
                quant_w(k + 2)
            if k + 3 < STEPS:
                prep_w(k + 3)
            if k + 1 < STEPS:
                prep_x(k + 1)
            for b in range(BLOCKS):
                first_product(k, b)
                if k == 0 and b == 0:
                    prep_pw(1, (nc.scalar.copy, nc.scalar.copy))
                if b == 2:
                    quant_y(k, 0, 2)
            if k >= HALVES and k % HALVES == 0:
                second_product(k // HALVES - 1, 0, BLOCKS)
            if k == 1:
                p1_bank = transpose_words([words(p1_raw[:], h, u) for h in range(HALVES) for u in range(PAIR)])
                nc.scalar.copy(
                    out=p1_grouped[:],
                    in_=p1_bank[:].rearrange("p (h u r) -> p h r u", h=HALVES, u=PAIR),
                )
                quantise(
                    p1_grouped[:].rearrange("p h r u -> p (h r u)").bitcast(BF16),
                    p1_codes[:].rearrange("p h r -> p (h r)"),
                    p1_scales[:].rearrange("p h r -> p (h r)"),
                )
            if k == 0:
                quant_pw(1, 0)
                quant_pw(1, 1)
        second_product(CHUNKS - 1, 0, 2)
        quant_y(STEPS - 1, 2, 3)
        quant_y(STEPS - 1, 3, 4)
        second_product(CHUNKS - 1, 2, 3)
        second_product(CHUNKS - 1, 3, 4)
